import numpy as np
import ml_dtypes


def mxq(x, axis, fmt="e4m3"):
    dtype, down = {"e4m3": (ml_dtypes.float8_e4m3fn, 7), "e5m2": (ml_dtypes.float8_e5m2, 14)}[fmt]
    v = np.moveaxis(np.asarray(x, np.float32).astype(ml_dtypes.bfloat16).astype(np.float64), axis, -1)
    blocks = v.reshape(v.shape[:-1] + (-1, 32))
    amax = np.abs(blocks).max(-1, keepdims=True)
    byte = np.maximum(np.where(amax > 0, np.frexp(amax)[1] - 1 + 127, 0) - down, 1)
    scale = np.exp2(byte - 127.0)
    codes = (blocks / scale).astype(np.float32).astype(dtype).astype(np.float64)
    return np.moveaxis((codes * scale).reshape(v.shape), -1, axis)


WIDE = False


def mx_kscale(k):
    if not WIDE:
        return np.ones(k)
    levels = np.array([10, -10, 5, -5, 0])
    if k % 512:
        return np.exp2(np.random.permutation(np.resize(levels, k // 32))).repeat(32)
    a = np.empty((k // 512, 16))
    for p in range(k // 512):
        a[p, :8] = np.random.permutation(np.resize(levels, 8))
        for g in range(8):
            far = levels[np.abs(levels - a[p, g]) >= 10]
            a[p, g + 8] = far[np.random.randint(len(far))]
    return np.exp2(a.ravel()).repeat(32)


BF16 = ml_dtypes.bfloat16


def bf(x):
    return np.asarray(x, np.float32).astype(BF16)


def f64(x):
    return np.asarray(x).astype(np.float64)


B, S, D, H, DK, F = 2, 256, 1024, 8, 128, 2560
HD = H * DK
EPS = 1e-6


def rmsnorm(v, g):
    return v / np.sqrt(np.mean(v * v, axis=-1, keepdims=True) + EPS) * g


def silu(v):
    return v / (1.0 + np.exp(-v))


def setup_inputs():
    s, t = mx_kscale(HD), mx_kscale(D)
    return {"x": bf(np.random.standard_normal((B, S, D))),
            "ao": bf(np.random.standard_normal((B, H, S, DK)) * 0.3 * s.reshape(H, 1, DK)),
            "wo": bf(np.random.standard_normal((HD, D)) * 1.5 / np.sqrt(HD) / s[:, None]),
            "bo": bf(np.random.standard_normal(D) * 0.1),
            "g2": bf((1.0 + 0.1 * np.random.standard_normal(D)) * t),
            "w1": bf(np.random.standard_normal((D, F)) / np.sqrt(D) / t[:, None]),
            "w3": bf(np.random.standard_normal((D, F)) / np.sqrt(D) / t[:, None])}


def reference(x, ao, wo, bo, g2, w1, w3):
    a = f64(ao).transpose(0, 2, 1, 3).reshape(B, S, HD)
    x1 = f64(x) + ((mxq(a, 2, "e4m3") @ mxq(f64(wo), 0, "e4m3")) + f64(bo))
    n = mxq(rmsnorm(x1, f64(g2)), 2, "e4m3")
    h = silu(n @ mxq(f64(w1), 0, "e4m3")) * (n @ mxq(f64(w3), 0, "e4m3"))
    return x1, h

@@ -1,0 +1,271 @@
+from contextlib import ExitStack
+
+import concourse.mybir as mybir
+from concourse.masks import make_identity
+
+F32 = mybir.dt.float32
+BF16 = mybir.dt.bfloat16
+U32 = mybir.dt.uint32
+U8 = mybir.dt.uint8
+I32 = mybir.dt.int32
+FP8X4 = mybir.dt.float8_e4m3fn_x4
+ACT = mybir.ActivationFunctionType
+ALU = mybir.AluOpType
+
+B, S, D, H, DK, F = 2, 256, 1024, 8, 128, 2560
+EPS = 1e-6
+
+P = 128
+WORDS = 2
+PACK = 4
+K_PASS = P * PACK
+PASSES = D // K_PASS
+N_TILE = 512
+TAIL_TILE = 256
+SLAB_COLS = 1024
+H_BUFS = 8
+RAW_BUFS = 4
+SCALAR_COLS = 256
+
+FLOPS = 2 * B * S * D * (D + 2 * F)
+
+
+def tile_transformerblock_pb_kernel(tc, x, ao, wo, bo, g2, w1, w3, out_0, out_1):
+    nc = tc.nc
+
+    token_tiles = [(b, i) for b in range(B) for i in range(2)]
+    ao_rows = ao.rearrange("b h (p i) d -> b i p h d", i=2)
+    x_rows = x.rearrange("b (p i) d -> b p (i d)", i=2)
+    x1_rows = out_0.rearrange("b (p i) d -> b i p d", i=2)
+    h_rows = out_1.rearrange("b (p i) f -> b i p f", i=2)
+
+    groups = [[(wo, 0, D)]]
+    for c0 in range(0, F, SLAB_COLS):
+        groups.append([(w, c0, min(SLAB_COLS, F - c0)) for w in (w1, w3)])
+    piece_cols = [N_TILE] * (len(groups) - 1) + [TAIL_TILE]
+    pieces = [
+        (q, g, c, j)
+        for q in range(len(groups))
+        for g in range(PASSES)
+        for c in range(0, groups[q][0][2], piece_cols[q])
+        for j in range(len(groups[q]))
+    ]
+
+    with ExitStack() as ctx:
+        const = ctx.enter_context(tc.tile_pool(name="const", bufs=1))
+        acts = ctx.enter_context(tc.tile_pool(name="acts", bufs=1))
+        raw_pool = ctx.enter_context(tc.tile_pool(name="raw", bufs=RAW_BUFS))
+        grouped_pool = ctx.enter_context(tc.tile_pool(name="grouped", bufs=4))
+        mx_pool = ctx.enter_context(tc.tile_pool(name="mx", bufs=1))
+        work = ctx.enter_context(tc.tile_pool(name="work", bufs=2))
+        out_pool = ctx.enter_context(tc.tile_pool(name="out", bufs=4))
+        psum = ctx.enter_context(tc.psum_pool(name="psum", bufs=8))
+
+        raw_slabs = {}
+        grouped_pieces = {}
+        piece_codes = {}
+        piece_scales = {}
+        progress = {"steps": 0}
+
+        def load_group(q):
+            for j in range(len(groups[q])):
+                raw_slabs[(q, j)] = raw_pool.tile(
+                    [P, PASSES, PACK, SLAB_COLS], BF16, tag="raw", name="raw%d_%d" % (q, j)
+                )
+            for g in range(PASSES):
+                for j, (w, c0, width) in enumerate(groups[q]):
+                    rows = w.rearrange("(g p t) n -> g p t n", g=PASSES, t=PACK)
+                    nc.sync.dma_start(
+                        out=raw_slabs[(q, j)][:, g, :, :width], in_=rows[g][:, :, c0 : c0 + width]
+                    )
+
+        def regroup(k):
+            q, g, c, j = pieces[k]
+            cols = piece_cols[q]
+            scalar_cols = cols * SCALAR_COLS // N_TILE
+            grouped = grouped_pool.tile([P, N_TILE, PACK], BF16, align_bytes=64)
+            for copy, lo, hi in (
+                (nc.scalar.copy, 0, scalar_cols),
+                (nc.vector.tensor_copy, scalar_cols, cols),
+            ):
+                copy(
+                    out=grouped[:, lo:hi, :].rearrange("p (c i) t -> p c t i", i=4),
+                    in_=raw_slabs[(q, j)][:, g, :, c + lo : c + hi].rearrange("p t (c i) -> p c t i", i=4),
+                )
+            grouped_pieces[k] = grouped
+            last_of_group = k + 1 == len(pieces) or pieces[k + 1][0] != q
+            if last_of_group and q + 2 < len(groups):
+                load_group(q + 2)
+
+        def quantise(k):
+            cols = piece_cols[pieces[k][0]]
+            codes = mx_pool.tile([P, cols], U32, name="codes%d" % k, align_bytes=64)
+            scales = mx_pool.tile([P, cols], U8, name="scales%d" % k, align_bytes=64)
+            nc.vector.quantize_mx(
+                out=codes[:].bitcast(FP8X4),
+                scales=scales[:],
+                in_=grouped_pieces[k][:, :cols, :].rearrange("p w t -> p (w t)"),
+            )
+            piece_codes[pieces[k]] = codes
+            piece_scales[pieces[k]] = scales
+
+        def weight_step():
+            k = progress["steps"]
+            if k < len(pieces):
+                regroup(k)
+            if 1 <= k <= len(pieces):
+                quantise(k - 1)
+            progress["steps"] = k + 1
+
+        def transpose_words(rows):
+            words = rows.bitcast(F32)
+            flipped = psum.tile([P, PASSES, WORDS, P], F32, tag="bank")
+            for g in range(PASSES):
+                for u in range(WORDS):
+                    nc.tensor.transpose(
+                        out=flipped[:, g, u, :],
+                        in_=words[:, K_PASS // 2 * g + u : K_PASS // 2 * (g + 1) : WORDS],
+                        identity=ident[:],
+                    )
+            return flipped
+
+        def group_words(flipped):
+            grouped_act = work.tile([P, PASSES, P, PACK], BF16, align_bytes=64, bufs=len(token_tiles))
+            nc.scalar.copy(
+                out=grouped_act[:]
+                .rearrange("p g r t -> p (g r t)")
+                .bitcast(F32)
+                .rearrange("p (g r u) -> p g r u", g=PASSES, u=WORDS),
+                in_=flipped[:].rearrange("p g u r -> p g r u"),
+            )
+            return grouped_act
+
+        def quantise_tokens(grouped_act, codes, scales):
+            nc.vector.quantize_mx(
+                out=codes.rearrange("p g r -> p (g r)").bitcast(FP8X4),
+                scales=scales.rearrange("p g r -> p (g r)"),
+                in_=grouped_act[:].rearrange("p g r t -> p (g r t)"),
+            )
+
+        def one_pass(acc, act_codes, act_scales, m, q, g, c, j):
+            nc.tensor.matmul_mx(
+                out=acc[:],
+                lhsT=act_codes[:, m, g, :].bitcast(FP8X4),
+                lhsT_scale=act_scales[:, m, g, :],
+                rhs=piece_codes[(q, g, c, j)][:].bitcast(FP8X4),
+                rhs_scale=piece_scales[(q, g, c, j)][:],
+                start=(g == 0),
+                stop=(g == PASSES - 1),
+            )
+
+        vectors = const.tile([P, 2 * D], BF16)
+        nc.vector.memset(vectors[:].bitcast(I32), 0)
+        ones = const.tile([P, P], BF16)
+        nc.vector.memset(ones[:], 1.0)
+        ident = const.tile([P, P], F32)
+        make_identity(nc, ident[:])
+        eps = const.tile([P, 1], F32)
+        nc.vector.memset(eps[:], EPS)
+        warm = const.tile([P, 1], F32)
+        nc.scalar.activation(out=warm[:], in_=eps[:], func=ACT.Sqrt)
+
+        a_sb = acts.tile([P, B, 2, H, DK], BF16)
+        x_sb = acts.tile([P, B, 2, D], BF16)
+        for b in range(B):
+            for i in range(2):
+                nc.sync.dma_start(out=a_sb[:, b, i], in_=ao_rows[b, i])
+            if b == 0:
+                nc.sync.dma_start(out=vectors[0:1, :D], in_=bo.rearrange("(o d) -> o d", o=1))
+                nc.sync.dma_start(out=vectors[0:1, D:], in_=g2.rearrange("(o d) -> o d", o=1))
+            nc.sync.dma_start(out=x_sb[:, b].rearrange("p i d -> p (i d)"), in_=x_rows[b])
+        load_group(0)
+        load_group(1)
+
+        summed = {}
+        for c in range(0, 2 * D, N_TILE):
+            summed[c] = psum.tile([P, N_TILE], F32, tag="bank", name="summed%d" % c)
+            nc.tensor.matmul(
+                out=summed[c][:], lhsT=ones[:], rhs=vectors[:, c : c + N_TILE], start=True, stop=True
+            )
+
+        x1 = []
+        for m, (b, i) in enumerate(token_tiles):
+            x1_m = acts.tile([P, D], F32, name="x1_%d" % m)
+            x1.append(x1_m)
+            for c in range(0, D, N_TILE):
+                nc.vector.tensor_tensor(
+                    out=x1_m[:, c : c + N_TILE], in0=summed[c][:], in1=x_sb[:, b, i, c : c + N_TILE], op=ALU.add
+                )
+        a_codes = acts.tile([P, len(token_tiles), PASSES, P], U32, align_bytes=64)
+        a_scales = acts.tile([P, len(token_tiles), PASSES, P], U8, align_bytes=64)
+        for m, (b, i) in enumerate(token_tiles):
+            grouped_a = group_words(transpose_words(a_sb[:, b, i].rearrange("p h d -> p (h d)")))
+            quantise_tokens(grouped_a, a_codes[:, m], a_scales[:, m])
+        g2_all = const.tile([P, D], BF16)
+        for c in range(0, D, N_TILE):
+            nc.scalar.copy(out=g2_all[:, c : c + N_TILE], in_=summed[D + c][:])
+
+        acc = {}
+        for g in range(PASSES):
+            for k in range(D // N_TILE + (1 if g == 0 else 0)):
+                weight_step()
+            for m in range(len(token_tiles)):
+                for c in range(0, D, N_TILE):
+                    if g == 0:
+                        acc[(m, c)] = psum.tile([P, N_TILE], F32, tag="bank", name="acc%d_%d" % (m, c))
+                    one_pass(acc[(m, c)], a_codes, a_scales, m, 0, g, c, 0)
+        weight_step()
+        sum_sq = const.tile([P, len(token_tiles)], F32)
+        for m, (b, i) in enumerate(token_tiles):
+            for c in range(0, D, N_TILE):
+                nc.vector.tensor_tensor(
+                    out=x1[m][:, c : c + N_TILE], in0=acc[(m, c)][:], in1=x1[m][:, c : c + N_TILE], op=ALU.add
+                )
+            nc.sync.dma_start(out=x1_rows[b, i], in_=x1[m][:])
+            squares = work.tile([P, D], BF16)
+            nc.scalar.activation(
+                out=squares[:], in_=x1[m][:], func=ACT.Square, accum_out=sum_sq[:, m : m + 1]
+            )
+
+        rms = const.tile([P, len(token_tiles)], F32)
+        nc.scalar.activation(out=rms[:], in_=sum_sq[:], func=ACT.Sqrt, scale=1.0 / D, bias=eps[:])
+        weight_step()
+        inv_rms = const.tile([P, len(token_tiles)], F32)
+        nc.vector.reciprocal(out=inv_rms[:], in_=rms[:])
+        n_codes = acts.tile([P, len(token_tiles), PASSES, P], U32, align_bytes=64)
+        n_scales = acts.tile([P, len(token_tiles), PASSES, P], U8, align_bytes=64)
+        grouped_n = {}
+        for m in range(len(token_tiles) + 1):
+            if m < len(token_tiles):
+                n_sb = work.tile([P, D], BF16)
+                nc.vector.scalar_tensor_tensor(
+                    out=n_sb[:],
+                    in0=x1[m][:],
+                    scalar=inv_rms[:, m : m + 1],
+                    in1=g2_all[:],
+                    op0=ALU.mult,
+                    op1=ALU.mult,
+                )
+                flipped_n = transpose_words(n_sb[:])
+            weight_step()
+            if m < len(token_tiles):
+                grouped_n[m] = group_words(flipped_n)
+            if m > 0:
+                quantise_tokens(grouped_n[m - 1], n_codes[:, m - 1], n_scales[:, m - 1])
+
+        for q in range(1, len(groups)):
+            c0, width = groups[q][0][1], groups[q][0][2]
+            cols = piece_cols[q]
+            for c in range(0, width, cols):
+                for m, (b, i) in enumerate(token_tiles):
+                    u = psum.tile([P, cols], F32, tag="bank")
+                    v = psum.tile([P, cols], F32, tag="bank")
+                    for j, bank in enumerate((u, v)):
+                        for g in range(PASSES):
+                            one_pass(bank, n_codes, n_scales, m, q, g, c, j)
+                    gate = out_pool.tile([P, cols], F32)
+                    nc.scalar.activation(out=gate[:], in_=u[:], func=ACT.Silu)
+                    weight_step()
+                    h_sb = out_pool.tile([P, cols], F32, bufs=H_BUFS)
+                    nc.vector.tensor_tensor(out=h_sb[:], in0=v[:], in1=gate[:], op=ALU.mult)
+                    nc.sync.dma_start(out=h_rows[b, i][:, c0 + c : c0 + c + cols], in_=h_sb[:])

@@ -24,7 +24,7 @@ N_TILE = 512
 TAIL_TILE = 256
 SLAB_COLS = 1024
 H_BUFS = 8
-RAW_BUFS = 4
+RAW_BUFS = 8
 SCALAR_COLS = 256
 
 FLOPS = 2 * B * S * D * (D + 2 * F)
@@ -50,6 +50,13 @@ def tile_transformerblock_pb_kernel(tc, x, ao, wo, bo, g2, w1, w3, out_0, out_1)
         for c in range(0, groups[q][0][2], piece_cols[q])
         for j in range(len(groups[q]))
     ]
+    slabs = [(0, 0, 0, c, N_TILE) for c in range(0, D, N_TILE)] + [(0, 1, 0, 0, D)]
+    slabs += [
+        (q, g, j, 0, groups[q][j][2])
+        for q in range(1, len(groups))
+        for g in range(PASSES)
+        for j in range(len(groups[q]))
+    ]
 
     with ExitStack() as ctx:
         const = ctx.enter_context(tc.tile_pool(name="const", bufs=1))
@@ -65,37 +72,40 @@ def tile_transformerblock_pb_kernel(tc, x, ao, wo, bo, g2, w1, w3, out_0, out_1)
         grouped_pieces = {}
         piece_codes = {}
         piece_scales = {}
-        progress = {"steps": 0}
+        progress = {"steps": 0, "loads": 0}
 
-        def load_group(q):
-            for j in range(len(groups[q])):
-                raw_slabs[(q, j)] = raw_pool.tile(
-                    [P, PASSES, PACK, SLAB_COLS], BF16, tag="raw", name="raw%d_%d" % (q, j)
-                )
-            for g in range(PASSES):
-                for j, (w, c0, width) in enumerate(groups[q]):
-                    rows = w.rearrange("(g p t) n -> g p t n", g=PASSES, t=PACK)
-                    nc.sync.dma_start(
-                        out=raw_slabs[(q, j)][:, g, :, :width], in_=rows[g][:, :, c0 : c0 + width]
-                    )
+        def load_slabs(count):
+            for n in range(progress["loads"], min(progress["loads"] + count, len(slabs))):
+                q, g, j, lo, width = slabs[n]
+                w, c0 = groups[q][j][:2]
+                slab = raw_pool.tile([P, PACK, SLAB_COLS], BF16, tag="raw", name="raw%d" % n)
+                rows = w.rearrange("(g p t) n -> g p t n", g=PASSES, t=PACK)
+                nc.sync.dma_start(out=slab[:, :, :width], in_=rows[g][:, :, c0 + lo : c0 + lo + width])
+                raw_slabs[n] = slab
+                progress["loads"] = n + 1
+
+        def slab_of(piece):
+            q, g, c, j = piece
+            return [s[:3] == (q, g, j) and s[3] <= c < s[3] + s[4] for s in slabs].index(True)
 
         def regroup(k):
             q, g, c, j = pieces[k]
             cols = piece_cols[q]
             scalar_cols = cols * SCALAR_COLS // N_TILE
+            n = slab_of(pieces[k])
+            lo = c - slabs[n][3]
             grouped = grouped_pool.tile([P, N_TILE, PACK], BF16, align_bytes=64)
-            for copy, lo, hi in (
+            for copy, first, end in (
                 (nc.scalar.copy, 0, scalar_cols),
                 (nc.vector.tensor_copy, scalar_cols, cols),
             ):
                 copy(
-                    out=grouped[:, lo:hi, :].rearrange("p (c i) t -> p c t i", i=4),
-                    in_=raw_slabs[(q, j)][:, g, :, c + lo : c + hi].rearrange("p t (c i) -> p c t i", i=4),
+                    out=grouped[:, first:end, :].rearrange("p (c i) t -> p c t i", i=4),
+                    in_=raw_slabs[n][:, :, lo + first : lo + end].rearrange("p t (c i) -> p c t i", i=4),
                 )
             grouped_pieces[k] = grouped
-            last_of_group = k + 1 == len(pieces) or pieces[k + 1][0] != q
-            if last_of_group and q + 2 < len(groups):
-                load_group(q + 2)
+            if k + 1 == len(pieces) or n not in [slab_of(piece) for piece in pieces[k + 1 :]]:
+                load_slabs(1)
 
         def quantise(k):
             cols = piece_cols[pieces[k][0]]
@@ -171,15 +181,17 @@ def tile_transformerblock_pb_kernel(tc, x, ao, wo, bo, g2, w1, w3, out_0, out_1)
 
         a_sb = acts.tile([P, B, 2, H, DK], BF16)
         x_sb = acts.tile([P, B, 2, D], BF16)
+        load_slabs(2)
+        nc.sync.dma_start(out=vectors[0:1, :D], in_=bo.rearrange("(o d) -> o d", o=1))
+        nc.sync.dma_start(out=vectors[0:1, D:], in_=g2.rearrange("(o d) -> o d", o=1))
+        for b in range(B):
+            nc.sync.dma_start(out=x_sb[:, b].rearrange("p i d -> p (i d)"), in_=x_rows[b])
         for b in range(B):
             for i in range(2):
                 nc.sync.dma_start(out=a_sb[:, b, i], in_=ao_rows[b, i])
             if b == 0:
-                nc.sync.dma_start(out=vectors[0:1, :D], in_=bo.rearrange("(o d) -> o d", o=1))
-                nc.sync.dma_start(out=vectors[0:1, D:], in_=g2.rearrange("(o d) -> o d", o=1))
-            nc.sync.dma_start(out=x_sb[:, b].rearrange("p i d -> p (i d)"), in_=x_rows[b])
-        load_group(0)
-        load_group(1)
+                load_slabs(1)
+        load_slabs(RAW_BUFS - 3)
 
         summed = {}
         for c in range(0, 2 * D, N_TILE):
@@ -188,6 +200,8 @@ def tile_transformerblock_pb_kernel(tc, x, ao, wo, bo, g2, w1, w3, out_0, out_1)
                 out=summed[c][:], lhsT=ones[:], rhs=vectors[:, c : c + N_TILE], start=True, stop=True
             )
 
+        weight_step()
+        weight_step()
         x1 = []
         for m, (b, i) in enumerate(token_tiles):
             x1_m = acts.tile([P, D], F32, name="x1_%d" % m)
@@ -207,7 +221,7 @@ def tile_transformerblock_pb_kernel(tc, x, ao, wo, bo, g2, w1, w3, out_0, out_1)
 
         acc = {}
         for g in range(PASSES):
-            for k in range(D // N_TILE + (1 if g == 0 else 0)):
+            for k in range(1 if g == 0 else 2):
                 weight_step()
             for m in range(len(token_tiles)):
                 for c in range(0, D, N_TILE):

@@ -24,8 +24,8 @@ N_TILE = 512
 TAIL_TILE = 256
 SLAB_COLS = 1024
 H_BUFS = 8
-RAW_BUFS = 8
-SCALAR_COLS = 256
+RAW_BUFS = 7
+SCALAR_COLS = 288
 
 FLOPS = 2 * B * S * D * (D + 2 * F)
 
@@ -42,14 +42,6 @@ def tile_transformerblock_pb_kernel(tc, x, ao, wo, bo, g2, w1, w3, out_0, out_1)
     groups = [[(wo, 0, D)]]
     for c0 in range(0, F, SLAB_COLS):
         groups.append([(w, c0, min(SLAB_COLS, F - c0)) for w in (w1, w3)])
-    piece_cols = [N_TILE] * (len(groups) - 1) + [TAIL_TILE]
-    pieces = [
-        (q, g, c, j)
-        for q in range(len(groups))
-        for g in range(PASSES)
-        for c in range(0, groups[q][0][2], piece_cols[q])
-        for j in range(len(groups[q]))
-    ]
     slabs = [(0, 0, 0, c, N_TILE) for c in range(0, D, N_TILE)] + [(0, 1, 0, 0, D)]
     slabs += [
         (q, g, j, 0, groups[q][j][2])
@@ -57,12 +49,17 @@ def tile_transformerblock_pb_kernel(tc, x, ao, wo, bo, g2, w1, w3, out_0, out_1)
         for g in range(PASSES)
         for j in range(len(groups[q]))
     ]
+    pieces = [(n, 0, slabs[n][4]) for n in range(len(slabs)) if slabs[n][0] < len(groups) - 1]
+    last_slabs = [n for n in range(len(slabs)) if slabs[n][0] == len(groups) - 1]
+    for g in range(PASSES):
+        for c in range(0, groups[-1][0][2], TAIL_TILE):
+            pieces += [(n, c, TAIL_TILE) for n in last_slabs if slabs[n][1] == g]
 
     with ExitStack() as ctx:
         const = ctx.enter_context(tc.tile_pool(name="const", bufs=1))
         acts = ctx.enter_context(tc.tile_pool(name="acts", bufs=1))
         raw_pool = ctx.enter_context(tc.tile_pool(name="raw", bufs=RAW_BUFS))
-        grouped_pool = ctx.enter_context(tc.tile_pool(name="grouped", bufs=4))
+        grouped_pool = ctx.enter_context(tc.tile_pool(name="grouped", bufs=3))
         mx_pool = ctx.enter_context(tc.tile_pool(name="mx", bufs=1))
         work = ctx.enter_context(tc.tile_pool(name="work", bufs=2))
         out_pool = ctx.enter_context(tc.tile_pool(name="out", bufs=4))
@@ -70,8 +67,8 @@ def tile_transformerblock_pb_kernel(tc, x, ao, wo, bo, g2, w1, w3, out_0, out_1)
 
         raw_slabs = {}
         grouped_pieces = {}
-        piece_codes = {}
-        piece_scales = {}
+        weight_codes = {}
+        weight_scales = {}
         progress = {"steps": 0, "loads": 0}
 
         def load_slabs(count):
@@ -84,40 +81,36 @@ def tile_transformerblock_pb_kernel(tc, x, ao, wo, bo, g2, w1, w3, out_0, out_1)
                 raw_slabs[n] = slab
                 progress["loads"] = n + 1
 
-        def slab_of(piece):
-            q, g, c, j = piece
-            return [s[:3] == (q, g, j) and s[3] <= c < s[3] + s[4] for s in slabs].index(True)
-
         def regroup(k):
-            q, g, c, j = pieces[k]
-            cols = piece_cols[q]
-            scalar_cols = cols * SCALAR_COLS // N_TILE
-            n = slab_of(pieces[k])
-            lo = c - slabs[n][3]
-            grouped = grouped_pool.tile([P, N_TILE, PACK], BF16, align_bytes=64)
+            n, lo, width = pieces[k]
+            scalar_cols = width * SCALAR_COLS // N_TILE
+            grouped = grouped_pool.tile([P, SLAB_COLS, PACK], BF16, align_bytes=64)
             for copy, first, end in (
                 (nc.scalar.copy, 0, scalar_cols),
-                (nc.vector.tensor_copy, scalar_cols, cols),
+                (nc.vector.tensor_copy, scalar_cols, width),
             ):
                 copy(
                     out=grouped[:, first:end, :].rearrange("p (c i) t -> p c t i", i=4),
                     in_=raw_slabs[n][:, :, lo + first : lo + end].rearrange("p t (c i) -> p c t i", i=4),
                 )
             grouped_pieces[k] = grouped
-            if k + 1 == len(pieces) or n not in [slab_of(piece) for piece in pieces[k + 1 :]]:
+            if n not in [piece[0] for piece in pieces[k + 1 :]]:
                 load_slabs(1)
 
         def quantise(k):
-            cols = piece_cols[pieces[k][0]]
-            codes = mx_pool.tile([P, cols], U32, name="codes%d" % k, align_bytes=64)
-            scales = mx_pool.tile([P, cols], U8, name="scales%d" % k, align_bytes=64)
+            n, lo, width = pieces[k]
+            codes = mx_pool.tile([P, width], U32, name="codes%d" % k, align_bytes=64)
+            scales = mx_pool.tile([P, width], U8, name="scales%d" % k, align_bytes=64)
             nc.vector.quantize_mx(
                 out=codes[:].bitcast(FP8X4),
                 scales=scales[:],
-                in_=grouped_pieces[k][:, :cols, :].rearrange("p w t -> p (w t)"),
+                in_=grouped_pieces[k][:, :width, :].rearrange("p w t -> p (w t)"),
             )
-            piece_codes[pieces[k]] = codes
-            piece_scales[pieces[k]] = scales
+            q, g, j, c = slabs[n][:4]
+            for part in range(0, width, N_TILE):
+                part_cols = slice(part, min(part + N_TILE, width))
+                weight_codes[(q, g, j, c + lo + part)] = codes[:, part_cols]
+                weight_scales[(q, g, j, c + lo + part)] = scales[:, part_cols]
 
         def weight_step():
             k = progress["steps"]
@@ -162,8 +155,8 @@ def tile_transformerblock_pb_kernel(tc, x, ao, wo, bo, g2, w1, w3, out_0, out_1)
                 out=acc[:],
                 lhsT=act_codes[:, m, g, :].bitcast(FP8X4),
                 lhsT_scale=act_scales[:, m, g, :],
-                rhs=piece_codes[(q, g, c, j)][:].bitcast(FP8X4),
-                rhs_scale=piece_scales[(q, g, c, j)][:],
+                rhs=weight_codes[(q, g, j, c)].bitcast(FP8X4),
+                rhs_scale=weight_scales[(q, g, j, c)],
                 start=(g == 0),
                 stop=(g == PASSES - 1),
             )
@@ -221,14 +214,12 @@ def tile_transformerblock_pb_kernel(tc, x, ao, wo, bo, g2, w1, w3, out_0, out_1)
 
         acc = {}
         for g in range(PASSES):
-            for k in range(1 if g == 0 else 2):
-                weight_step()
+            weight_step()
             for m in range(len(token_tiles)):
                 for c in range(0, D, N_TILE):
                     if g == 0:
                         acc[(m, c)] = psum.tile([P, N_TILE], F32, tag="bank", name="acc%d_%d" % (m, c))
                     one_pass(acc[(m, c)], a_codes, a_scales, m, 0, g, c, 0)
-        weight_step()
         sum_sq = const.tile([P, len(token_tiles)], F32)
         for m, (b, i) in enumerate(token_tiles):
             for c in range(0, D, N_TILE):
@@ -243,33 +234,29 @@ def tile_transformerblock_pb_kernel(tc, x, ao, wo, bo, g2, w1, w3, out_0, out_1)
 
         rms = const.tile([P, len(token_tiles)], F32)
         nc.scalar.activation(out=rms[:], in_=sum_sq[:], func=ACT.Sqrt, scale=1.0 / D, bias=eps[:])
-        weight_step()
         inv_rms = const.tile([P, len(token_tiles)], F32)
         nc.vector.reciprocal(out=inv_rms[:], in_=rms[:])
         n_codes = acts.tile([P, len(token_tiles), PASSES, P], U32, align_bytes=64)
         n_scales = acts.tile([P, len(token_tiles), PASSES, P], U8, align_bytes=64)
         grouped_n = {}
-        for m in range(len(token_tiles) + 1):
-            if m < len(token_tiles):
-                n_sb = work.tile([P, D], BF16)
-                nc.vector.scalar_tensor_tensor(
-                    out=n_sb[:],
-                    in0=x1[m][:],
-                    scalar=inv_rms[:, m : m + 1],
-                    in1=g2_all[:],
-                    op0=ALU.mult,
-                    op1=ALU.mult,
-                )
-                flipped_n = transpose_words(n_sb[:])
+        for m in range(len(token_tiles)):
+            n_sb = work.tile([P, D], BF16)
+            nc.vector.scalar_tensor_tensor(
+                out=n_sb[:],
+                in0=x1[m][:],
+                scalar=inv_rms[:, m : m + 1],
+                in1=g2_all[:],
+                op0=ALU.mult,
+                op1=ALU.mult,
+            )
+            grouped_n[m] = group_words(transpose_words(n_sb[:]))
+            quantise_tokens(grouped_n[m], n_codes[:, m], n_scales[:, m])
+        for k in range(4):
             weight_step()
-            if m < len(token_tiles):
-                grouped_n[m] = group_words(flipped_n)
-            if m > 0:
-                quantise_tokens(grouped_n[m - 1], n_codes[:, m - 1], n_scales[:, m - 1])
 
         for q in range(1, len(groups)):
-            c0, width = groups[q][0][1], groups[q][0][2]
-            cols = piece_cols[q]
+            c0, width = groups[q][0][1:]
+            cols = TAIL_TILE if q == len(groups) - 1 else N_TILE
             for c in range(0, width, cols):
                 for m, (b, i) in enumerate(token_tiles):
                     u = psum.tile([P, cols], F32, tag="bank")
@@ -279,7 +266,8 @@ def tile_transformerblock_pb_kernel(tc, x, ao, wo, bo, g2, w1, w3, out_0, out_1)
                             one_pass(bank, n_codes, n_scales, m, q, g, c, j)
                     gate = out_pool.tile([P, cols], F32)
                     nc.scalar.activation(out=gate[:], in_=u[:], func=ACT.Silu)
-                    weight_step()
+                    if q > 1 or m % 2 == 0:
+                        weight_step()
                     h_sb = out_pool.tile([P, cols], F32, bufs=H_BUFS)
                     nc.vector.tensor_tensor(out=h_sb[:], in0=v[:], in1=gate[:], op=ALU.mult)
                     nc.sync.dma_start(out=h_rows[b, i][:, c0 + c : c0 + c + cols], in_=h_sb[:])

@@ -26,6 +26,8 @@ SLAB_COLS = 1024
 H_BUFS = 8
 RAW_BUFS = 7
 SCALAR_COLS = 288
+TENSOR_COLS = 256
+BANK_COLS = 256
 
 FLOPS = 2 * B * S * D * (D + 2 * F)
 
@@ -83,12 +85,25 @@ def tile_transformerblock_pb_kernel(tc, x, ao, wo, bo, g2, w1, w3, out_0, out_1)
 
         def regroup(k):
             n, lo, width = pieces[k]
-            scalar_cols = width * SCALAR_COLS // N_TILE
+            by_tensor = slabs[n][0] == 1
+            scalar_cols = width * (TENSOR_COLS if by_tensor else SCALAR_COLS) // N_TILE
             grouped = grouped_pool.tile([P, SLAB_COLS, PACK], BF16, align_bytes=64)
-            for copy, first, end in (
-                (nc.scalar.copy, 0, scalar_cols),
-                (nc.vector.tensor_copy, scalar_cols, width),
-            ):
+            copies = [(nc.vector.tensor_copy, scalar_cols, width)]
+            if by_tensor:
+                for first in range(0, scalar_cols, BANK_COLS):
+                    bank = psum.tile([P, BANK_COLS, PACK], BF16, tag="pair", bufs=2)
+                    for part in range(0, BANK_COLS, P):
+                        nc.tensor.matmul(
+                            out=bank[:, part : part + P, :].rearrange("p c t -> p t c"),
+                            lhsT=ident_bf16[:],
+                            rhs=raw_slabs[n][:, :, lo + first + part : lo + first + part + P],
+                            start=True,
+                            stop=True,
+                        )
+                    nc.scalar.copy(out=grouped[:, first : first + BANK_COLS, :], in_=bank[:])
+            else:
+                copies.append((nc.scalar.copy, 0, scalar_cols))
+            for copy, first, end in copies:
                 copy(
                     out=grouped[:, first:end, :].rearrange("p (c i) t -> p c t i", i=4),
                     in_=raw_slabs[n][:, :, lo + first : lo + end].rearrange("p t (c i) -> p c t i", i=4),
@@ -122,7 +137,7 @@ def tile_transformerblock_pb_kernel(tc, x, ao, wo, bo, g2, w1, w3, out_0, out_1)
 
         def transpose_words(rows):
             words = rows.bitcast(F32)
-            flipped = psum.tile([P, PASSES, WORDS, P], F32, tag="bank")
+            flipped = psum.tile([P, PASSES, WORDS, P], F32, tag="bank", bufs=6)
             for g in range(PASSES):
                 for u in range(WORDS):
                     nc.tensor.transpose(
@@ -167,6 +182,8 @@ def tile_transformerblock_pb_kernel(tc, x, ao, wo, bo, g2, w1, w3, out_0, out_1)
         nc.vector.memset(ones[:], 1.0)
         ident = const.tile([P, P], F32)
         make_identity(nc, ident[:])
+        ident_bf16 = const.tile([P, P], BF16)
+        make_identity(nc, ident_bf16[:])
         eps = const.tile([P, 1], F32)
         nc.vector.memset(eps[:], EPS)
         warm = const.tile([P, 1], F32)
@@ -188,7 +205,7 @@ def tile_transformerblock_pb_kernel(tc, x, ao, wo, bo, g2, w1, w3, out_0, out_1)
 
         summed = {}
         for c in range(0, 2 * D, N_TILE):
-            summed[c] = psum.tile([P, N_TILE], F32, tag="bank", name="summed%d" % c)
+            summed[c] = psum.tile([P, N_TILE], F32, tag="bank", bufs=6, name="summed%d" % c)
             nc.tensor.matmul(
                 out=summed[c][:], lhsT=ones[:], rhs=vectors[:, c : c + N_TILE], start=True, stop=True
             )
@@ -212,19 +229,16 @@ def tile_transformerblock_pb_kernel(tc, x, ao, wo, bo, g2, w1, w3, out_0, out_1)
         for c in range(0, D, N_TILE):
             nc.scalar.copy(out=g2_all[:, c : c + N_TILE], in_=summed[D + c][:])
 
-        acc = {}
-        for g in range(PASSES):
+        for k in range(2):
             weight_step()
-            for m in range(len(token_tiles)):
-                for c in range(0, D, N_TILE):
-                    if g == 0:
-                        acc[(m, c)] = psum.tile([P, N_TILE], F32, tag="bank", name="acc%d_%d" % (m, c))
-                    one_pass(acc[(m, c)], a_codes, a_scales, m, 0, g, c, 0)
         sum_sq = const.tile([P, len(token_tiles)], F32)
         for m, (b, i) in enumerate(token_tiles):
             for c in range(0, D, N_TILE):
+                acc = psum.tile([P, N_TILE], F32, tag="bank", bufs=6)
+                for g in range(PASSES):
+                    one_pass(acc, a_codes, a_scales, m, 0, g, c, 0)
                 nc.vector.tensor_tensor(
-                    out=x1[m][:, c : c + N_TILE], in0=acc[(m, c)][:], in1=x1[m][:, c : c + N_TILE], op=ALU.add
+                    out=x1[m][:, c : c + N_TILE], in0=acc[:], in1=x1[m][:, c : c + N_TILE], op=ALU.add
                 )
             nc.sync.dma_start(out=x1_rows[b, i], in_=x1[m][:])
             squares = work.tile([P, D], BF16)
@@ -259,8 +273,9 @@ def tile_transformerblock_pb_kernel(tc, x, ao, wo, bo, g2, w1, w3, out_0, out_1)
             cols = TAIL_TILE if q == len(groups) - 1 else N_TILE
             for c in range(0, width, cols):
                 for m, (b, i) in enumerate(token_tiles):
-                    u = psum.tile([P, cols], F32, tag="bank")
-                    v = psum.tile([P, cols], F32, tag="bank")
+                    tag, bufs = ("pair", 2) if m == len(token_tiles) - 1 else ("bank", 6)
+                    u = psum.tile([P, cols], F32, tag=tag, bufs=bufs)
+                    v = psum.tile([P, cols], F32, tag=tag, bufs=bufs)
                     for j, bank in enumerate((u, v)):
                         for g in range(PASSES):
                             one_pass(bank, n_codes, n_scales, m, q, g, c, j)

from contextlib import ExitStack

import concourse.mybir as mybir
from concourse.masks import make_identity

F32 = mybir.dt.float32
BF16 = mybir.dt.bfloat16
U32 = mybir.dt.uint32
U8 = mybir.dt.uint8
I32 = mybir.dt.int32
FP8X4 = mybir.dt.float8_e4m3fn_x4
ACT = mybir.ActivationFunctionType
ALU = mybir.AluOpType

B, S, D, H, DK, F = 2, 256, 1024, 8, 128, 2560
EPS = 1e-6

P = 128
WORDS = 2
PACK = 4
K_PASS = P * PACK
PASSES = D // K_PASS
N_TILE = 512
TAIL_TILE = 256
SLAB_COLS = 1024
H_BUFS = 8
RAW_BUFS = 7
SCALAR_COLS = 288
TENSOR_COLS = 256
BANK_COLS = 256

FLOPS = 2 * B * S * D * (D + 2 * F)


def tile_transformerblock_pb_kernel(tc, x, ao, wo, bo, g2, w1, w3, out_0, out_1):
    nc = tc.nc

    token_tiles = [(b, i) for b in range(B) for i in range(2)]
    ao_rows = ao.rearrange("b h (p i) d -> b i p h d", i=2)
    x_rows = x.rearrange("b (p i) d -> b p (i d)", i=2)
    x1_rows = out_0.rearrange("b (p i) d -> b i p d", i=2)
    h_rows = out_1.rearrange("b (p i) f -> b i p f", i=2)

    groups = [[(wo, 0, D)]]
    for c0 in range(0, F, SLAB_COLS):
        groups.append([(w, c0, min(SLAB_COLS, F - c0)) for w in (w1, w3)])
    slabs = [(0, 0, 0, c, N_TILE) for c in range(0, D, N_TILE)] + [(0, 1, 0, 0, D)]
    slabs += [
        (q, g, j, 0, groups[q][j][2])
        for q in range(1, len(groups))
        for g in range(PASSES)
        for j in range(len(groups[q]))
    ]
    pieces = [(n, 0, slabs[n][4]) for n in range(len(slabs)) if slabs[n][0] < len(groups) - 1]
    last_slabs = [n for n in range(len(slabs)) if slabs[n][0] == len(groups) - 1]
    for g in range(PASSES):
        for c in range(0, groups[-1][0][2], TAIL_TILE):
            pieces += [(n, c, TAIL_TILE) for n in last_slabs if slabs[n][1] == g]

    with ExitStack() as ctx:
        const = ctx.enter_context(tc.tile_pool(name="const", bufs=1))
        acts = ctx.enter_context(tc.tile_pool(name="acts", bufs=1))
        raw_pool = ctx.enter_context(tc.tile_pool(name="raw", bufs=RAW_BUFS))
        grouped_pool = ctx.enter_context(tc.tile_pool(name="grouped", bufs=3))
        mx_pool = ctx.enter_context(tc.tile_pool(name="mx", bufs=1))
        work = ctx.enter_context(tc.tile_pool(name="work", bufs=2))
        out_pool = ctx.enter_context(tc.tile_pool(name="out", bufs=4))
        psum = ctx.enter_context(tc.psum_pool(name="psum", bufs=8))

        raw_slabs = {}
        grouped_pieces = {}
        weight_codes = {}
        weight_scales = {}
        progress = {"steps": 0, "loads": 0}

        def load_slabs(count):
            for n in range(progress["loads"], min(progress["loads"] + count, len(slabs))):
                q, g, j, lo, width = slabs[n]
                w, c0 = groups[q][j][:2]
                slab = raw_pool.tile([P, PACK, SLAB_COLS], BF16, tag="raw", name="raw%d" % n)
                rows = w.rearrange("(g p t) n -> g p t n", g=PASSES, t=PACK)
                nc.sync.dma_start(out=slab[:, :, :width], in_=rows[g][:, :, c0 + lo : c0 + lo + width])
                raw_slabs[n] = slab
                progress["loads"] = n + 1

        def regroup(k):
            n, lo, width = pieces[k]
            by_tensor = slabs[n][0] == 1
            scalar_cols = width * (TENSOR_COLS if by_tensor else SCALAR_COLS) // N_TILE
            grouped = grouped_pool.tile([P, SLAB_COLS, PACK], BF16, align_bytes=64)
            copies = [(nc.vector.tensor_copy, scalar_cols, width)]
            if by_tensor:
                for first in range(0, scalar_cols, BANK_COLS):
                    bank = psum.tile([P, BANK_COLS, PACK], BF16, tag="pair", bufs=2)
                    for part in range(0, BANK_COLS, P):
                        nc.tensor.matmul(
                            out=bank[:, part : part + P, :].rearrange("p c t -> p t c"),
                            lhsT=ident_bf16[:],
                            rhs=raw_slabs[n][:, :, lo + first + part : lo + first + part + P],
                            start=True,
                            stop=True,
                        )
                    nc.scalar.copy(out=grouped[:, first : first + BANK_COLS, :], in_=bank[:])
            else:
                copies.append((nc.scalar.copy, 0, scalar_cols))
            for copy, first, end in copies:
                copy(
                    out=grouped[:, first:end, :].rearrange("p (c i) t -> p c t i", i=4),
                    in_=raw_slabs[n][:, :, lo + first : lo + end].rearrange("p t (c i) -> p c t i", i=4),
                )
            grouped_pieces[k] = grouped
            if n not in [piece[0] for piece in pieces[k + 1 :]]:
                load_slabs(1)

        def quantise(k):
            n, lo, width = pieces[k]
            codes = mx_pool.tile([P, width], U32, name="codes%d" % k, align_bytes=64)
            scales = mx_pool.tile([P, width], U8, name="scales%d" % k, align_bytes=64)
            nc.vector.quantize_mx(
                out=codes[:].bitcast(FP8X4),
                scales=scales[:],
                in_=grouped_pieces[k][:, :width, :].rearrange("p w t -> p (w t)"),
            )
            q, g, j, c = slabs[n][:4]
            for part in range(0, width, N_TILE):
                part_cols = slice(part, min(part + N_TILE, width))
                weight_codes[(q, g, j, c + lo + part)] = codes[:, part_cols]
                weight_scales[(q, g, j, c + lo + part)] = scales[:, part_cols]

        def weight_step():
            k = progress["steps"]
            if k < len(pieces):
                regroup(k)
            if 1 <= k <= len(pieces):
                quantise(k - 1)
            progress["steps"] = k + 1

        def transpose_words(rows):
            words = rows.bitcast(F32)
            flipped = psum.tile([P, PASSES, WORDS, P], F32, tag="bank", bufs=6)
            for g in range(PASSES):
                for u in range(WORDS):
                    nc.tensor.transpose(
                        out=flipped[:, g, u, :],
                        in_=words[:, K_PASS // 2 * g + u : K_PASS // 2 * (g + 1) : WORDS],
                        identity=ident[:],
                    )
            return flipped

        def group_words(flipped):
            grouped_act = work.tile([P, PASSES, P, PACK], BF16, align_bytes=64, bufs=len(token_tiles))
            nc.scalar.copy(
                out=grouped_act[:]
                .rearrange("p g r t -> p (g r t)")
                .bitcast(F32)
                .rearrange("p (g r u) -> p g r u", g=PASSES, u=WORDS),
                in_=flipped[:].rearrange("p g u r -> p g r u"),
            )
            return grouped_act

        def quantise_tokens(grouped_act, codes, scales):
            nc.vector.quantize_mx(
                out=codes.rearrange("p g r -> p (g r)").bitcast(FP8X4),
                scales=scales.rearrange("p g r -> p (g r)"),
                in_=grouped_act[:].rearrange("p g r t -> p (g r t)"),
            )

        def one_pass(acc, act_codes, act_scales, m, q, g, c, j):
            nc.tensor.matmul_mx(
                out=acc[:],
                lhsT=act_codes[:, m, g, :].bitcast(FP8X4),
                lhsT_scale=act_scales[:, m, g, :],
                rhs=weight_codes[(q, g, j, c)].bitcast(FP8X4),
                rhs_scale=weight_scales[(q, g, j, c)],
                start=(g == 0),
                stop=(g == PASSES - 1),
            )

        vectors = const.tile([P, 2 * D], BF16)
        nc.vector.memset(vectors[:].bitcast(I32), 0)
        ones = const.tile([P, P], BF16)
        nc.vector.memset(ones[:], 1.0)
        ident = const.tile([P, P], F32)
        make_identity(nc, ident[:])
        ident_bf16 = const.tile([P, P], BF16)
        make_identity(nc, ident_bf16[:])
        eps = const.tile([P, 1], F32)
        nc.vector.memset(eps[:], EPS)
        warm = const.tile([P, 1], F32)
        nc.scalar.activation(out=warm[:], in_=eps[:], func=ACT.Sqrt)

        a_sb = acts.tile([P, B, 2, H, DK], BF16)
        x_sb = acts.tile([P, B, 2, D], BF16)
        load_slabs(2)
        nc.sync.dma_start(out=vectors[0:1, :D], in_=bo.rearrange("(o d) -> o d", o=1))
        nc.sync.dma_start(out=vectors[0:1, D:], in_=g2.rearrange("(o d) -> o d", o=1))
        for b in range(B):
            nc.sync.dma_start(out=x_sb[:, b].rearrange("p i d -> p (i d)"), in_=x_rows[b])
        for b in range(B):
            for i in range(2):
                nc.sync.dma_start(out=a_sb[:, b, i], in_=ao_rows[b, i])
            if b == 0:
                load_slabs(1)
        load_slabs(RAW_BUFS - 3)

        summed = {}
        for c in range(0, 2 * D, N_TILE):
            summed[c] = psum.tile([P, N_TILE], F32, tag="bank", bufs=6, name="summed%d" % c)
            nc.tensor.matmul(
                out=summed[c][:], lhsT=ones[:], rhs=vectors[:, c : c + N_TILE], start=True, stop=True
            )

        weight_step()
        weight_step()
        x1 = []
        for m, (b, i) in enumerate(token_tiles):
            x1_m = acts.tile([P, D], F32, name="x1_%d" % m)
            x1.append(x1_m)
            for c in range(0, D, N_TILE):
                nc.vector.tensor_tensor(
                    out=x1_m[:, c : c + N_TILE], in0=summed[c][:], in1=x_sb[:, b, i, c : c + N_TILE], op=ALU.add
                )
        a_codes = acts.tile([P, len(token_tiles), PASSES, P], U32, align_bytes=64)
        a_scales = acts.tile([P, len(token_tiles), PASSES, P], U8, align_bytes=64)
        for m, (b, i) in enumerate(token_tiles):
            grouped_a = group_words(transpose_words(a_sb[:, b, i].rearrange("p h d -> p (h d)")))
            quantise_tokens(grouped_a, a_codes[:, m], a_scales[:, m])
        g2_all = const.tile([P, D], BF16)
        for c in range(0, D, N_TILE):
            nc.scalar.copy(out=g2_all[:, c : c + N_TILE], in_=summed[D + c][:])

        for k in range(2):
            weight_step()
        sum_sq = const.tile([P, len(token_tiles)], F32)
        for m, (b, i) in enumerate(token_tiles):
            for c in range(0, D, N_TILE):
                acc = psum.tile([P, N_TILE], F32, tag="bank", bufs=6)
                for g in range(PASSES):
                    one_pass(acc, a_codes, a_scales, m, 0, g, c, 0)
                nc.vector.tensor_tensor(
                    out=x1[m][:, c : c + N_TILE], in0=acc[:], in1=x1[m][:, c : c + N_TILE], op=ALU.add
                )
            nc.sync.dma_start(out=x1_rows[b, i], in_=x1[m][:])
            squares = work.tile([P, D], BF16)
            nc.scalar.activation(
                out=squares[:], in_=x1[m][:], func=ACT.Square, accum_out=sum_sq[:, m : m + 1]
            )

        rms = const.tile([P, len(token_tiles)], F32)
        nc.scalar.activation(out=rms[:], in_=sum_sq[:], func=ACT.Sqrt, scale=1.0 / D, bias=eps[:])
        inv_rms = const.tile([P, len(token_tiles)], F32)
        nc.vector.reciprocal(out=inv_rms[:], in_=rms[:])
        n_codes = acts.tile([P, len(token_tiles), PASSES, P], U32, align_bytes=64)
        n_scales = acts.tile([P, len(token_tiles), PASSES, P], U8, align_bytes=64)
        grouped_n = {}
        for m in range(len(token_tiles)):
            n_sb = work.tile([P, D], BF16)
            nc.vector.scalar_tensor_tensor(
                out=n_sb[:],
                in0=x1[m][:],
                scalar=inv_rms[:, m : m + 1],
                in1=g2_all[:],
                op0=ALU.mult,
                op1=ALU.mult,
            )
            grouped_n[m] = group_words(transpose_words(n_sb[:]))
            quantise_tokens(grouped_n[m], n_codes[:, m], n_scales[:, m])
        for k in range(4):
            weight_step()

        for q in range(1, len(groups)):
            c0, width = groups[q][0][1:]
            cols = TAIL_TILE if q == len(groups) - 1 else N_TILE
            for c in range(0, width, cols):
                for m, (b, i) in enumerate(token_tiles):
                    tag, bufs = ("pair", 2) if m == len(token_tiles) - 1 else ("bank", 6)
                    u = psum.tile([P, cols], F32, tag=tag, bufs=bufs)
                    v = psum.tile([P, cols], F32, tag=tag, bufs=bufs)
                    for j, bank in enumerate((u, v)):
                        for g in range(PASSES):
                            one_pass(bank, n_codes, n_scales, m, q, g, c, j)
                    gate = out_pool.tile([P, cols], F32)
                    nc.scalar.activation(out=gate[:], in_=u[:], func=ACT.Silu)
                    if q > 1 or m % 2 == 0:
                        weight_step()
                    h_sb = out_pool.tile([P, cols], F32, bufs=H_BUFS)
                    nc.vector.tensor_tensor(out=h_sb[:], in0=v[:], in1=gate[:], op=ALU.mult)
                    nc.sync.dma_start(out=h_rows[b, i][:, c0 + c : c0 + c + cols], in_=h_sb[:])
